import numpy as np
import ml_dtypes


def mxq(x, axis, fmt="e4m3"):
    dtype, down = {"e4m3": (ml_dtypes.float8_e4m3fn, 7), "e5m2": (ml_dtypes.float8_e5m2, 14)}[fmt]
    v = np.moveaxis(np.asarray(x, np.float32).astype(ml_dtypes.bfloat16).astype(np.float64), axis, -1)
    blocks = v.reshape(v.shape[:-1] + (-1, 32))
    amax = np.abs(blocks).max(-1, keepdims=True)
    byte = np.maximum(np.where(amax > 0, np.frexp(amax)[1] - 1 + 127, 0) - down, 1)
    scale = np.exp2(byte - 127.0)
    codes = (blocks / scale).astype(np.float32).astype(dtype).astype(np.float64)
    return np.moveaxis((codes * scale).reshape(v.shape), -1, axis)


WIDE = False


def mx_kscale(k):
    if not WIDE:
        return np.ones(k)
    levels = np.array([10, -10, 5, -5, 0])
    a = np.random.permutation(np.resize(levels, k // 512 * 4)).reshape(k // 512, 4)
    idx = np.arange(k)
    return np.exp2(a[idx // 512, idx % 128 // 32])


BF16 = ml_dtypes.bfloat16


def bf(x):
    return np.asarray(x, np.float32).astype(BF16)


def f64(x):
    return np.asarray(x).astype(np.float64)


E2M1 = np.array([0.0, 0.5, 1.0, 1.5, 2.0, 3.0, 4.0, 6.0, -0.0, -0.5, -1.0, -1.5, -2.0, -3.0, -4.0, -6.0])


def pack_weight(w, fmt):
    k, n = w.shape
    w = f64(bf(w)).reshape(k // 32, 32, n)
    amax = np.abs(w).max(1)
    if fmt == "e4m3":
        byte = np.frexp(amax)[1] - 1 + 127 - 7
    else:
        mant, ex = np.frexp(amax / 6.0)
        byte = np.where(mant > 0.5, ex, ex - 1) + 127
    byte = np.clip(np.where(amax > 0, byte, 1), 1, 254)
    scaled = (w * np.exp2(127.0 - byte)[:, None, :]).reshape(k, n).astype(np.float32)
    by_word = np.ascontiguousarray(scaled.reshape(k // 512, 128, 4, n).transpose(0, 1, 3, 2))
    if fmt == "e4m3":
        words = by_word.astype(ml_dtypes.float8_e4m3fn).view(np.uint8)
    else:
        c = by_word.astype(ml_dtypes.float4_e2m1fn).view(np.uint8) & 0xF
        words = c[..., 0::2] | (c[..., 1::2] << 4)
    return np.ascontiguousarray(words), np.ascontiguousarray(byte.astype(np.uint8).reshape(k // 512, 16, n))


def unpack_weight(words, scales, fmt):
    g, p, n, _ = words.shape
    if fmt == "e4m3":
        vals = np.ascontiguousarray(words).view(ml_dtypes.float8_e4m3fn).astype(np.float64)
    else:
        nib = np.empty((g, p, n, 4), np.uint8)
        nib[..., 0::2] = words & 0xF
        nib[..., 1::2] = words >> 4
        vals = E2M1[nib]
    vals = vals * np.repeat(np.exp2(scales.astype(np.float64) - 127.0), 8, axis=1)[..., None]
    return vals.transpose(0, 1, 3, 2).reshape(g * 512, n)


E, D_NODE, D_EDGE, D_GLOB, LATENT, D_OUT = 512, 4096, 4096, 4096, 512, 128
D_IN = D_NODE + D_NODE + D_EDGE + D_GLOB


def setup_inputs():
    s = mx_kscale(D_IN)
    o1 = D_NODE
    o2 = o1 + D_NODE
    o3 = o2 + D_EDGE
    receiver = bf(np.random.standard_normal((E, D_NODE)) * s[:o1])
    sender = bf(np.random.standard_normal((E, D_NODE)) * s[o1:o2])
    edge_attr = bf(np.random.standard_normal((E, D_EDGE)) * s[o2:o3])
    global_attr = bf(np.random.standard_normal((1, D_GLOB)) * s[o3:])
    W1_words, W1_scales = pack_weight(np.random.standard_normal((D_IN, LATENT)) / np.sqrt(D_IN) / s[:, None], "e4m3")
    b1 = bf(np.random.standard_normal(LATENT) * 0.1)
    return {
        "receiver": receiver,
        "sender": sender,
        "edge_attr": edge_attr,
        "global_attr": global_attr,
        "W1_words": W1_words,
        "W1_scales": W1_scales,
        "b1": b1,
    }


def reference(receiver, sender, edge_attr, global_attr, W1_words, W1_scales, b1):
    e = edge_attr.shape[0]
    g = np.tile(f64(global_attr), (e // global_attr.shape[0], 1))
    x = np.concatenate([f64(receiver), f64(sender), f64(edge_attr), g], axis=1)
    return np.maximum((mxq(x, 1, "e4m3") @ unpack_weight(W1_words, W1_scales, "e4m3")) + f64(b1), 0.0)

@@ -1,0 +1,226 @@
+from contextlib import ExitStack
+
+import concourse.mybir as mybir
+from concourse.masks import make_identity
+
+F32 = mybir.dt.float32
+BF16 = mybir.dt.bfloat16
+I32 = mybir.dt.int32
+U32 = mybir.dt.uint32
+U8 = mybir.dt.uint8
+FP8X4 = mybir.dt.float8_e4m3fn_x4
+
+P = 128
+PACK = 4
+GROUP_K = P * PACK
+GROUP_WORDS = GROUP_K // 2
+EDGES = 512
+EDGE_TILES = EDGES // P
+D_STREAM = 4096
+LATENT = 512
+STREAM_GROUPS = D_STREAM // GROUP_K
+X_GROUPS = 3 * STREAM_GROUPS
+ROUND_GROUPS = 2
+ROUND_K = ROUND_GROUPS * GROUP_K
+ROUNDS = X_GROUPS // ROUND_GROUPS
+STREAM_ROUNDS = STREAM_GROUPS // ROUND_GROUPS
+X_AHEAD = 5
+PLANES_PER_TILE = 4
+GLOB_LOAD_ROUND = 5
+GLOB_ROUND = 9
+
+FLOPS = 2 * EDGES * (4 * D_STREAM) * LATENT
+
+
+def tile_edgemodel_pa_k_kernel(
+    tc, receiver, sender, edge_attr, global_attr, W1_words, W1_scales, b1, out
+):
+    nc = tc.nc
+    streams = (receiver, sender, edge_attr)
+
+    with ExitStack() as ctx:
+        const = ctx.enter_context(tc.tile_pool(name="const", bufs=1))
+        weights = ctx.enter_context(tc.tile_pool(name="weights", bufs=1))
+        x_pool = ctx.enter_context(tc.tile_pool(name="x", bufs=X_AHEAD + 1))
+        grouped_pool = ctx.enter_context(tc.tile_pool(name="grouped", bufs=2))
+        quantised_pool = ctx.enter_context(tc.tile_pool(name="quantised", bufs=3))
+        result_pool = ctx.enter_context(tc.tile_pool(name="result", bufs=2))
+        sums_pool = ctx.enter_context(tc.psum_pool(name="sums", bufs=1))
+        bank_pool = ctx.enter_context(tc.psum_pool(name="bank", bufs=4))
+        ctx.enter_context(tc.manual_schedule())
+
+        identity = const.tile([P, P], F32)
+        make_identity(nc, identity[:])
+        ones = const.tile([P, P], BF16)
+        nc.vector.memset(ones[:], 1.0)
+        w_planes = const.tile([P, 4 * STREAM_GROUPS // PLANES_PER_TILE, LATENT], U8, align_bytes=64)
+        nc.vector.memset(w_planes[:].bitcast(I32), 0)
+        b_rows = const.tile([P, LATENT], BF16)
+        nc.vector.memset(b_rows[:].bitcast(I32), 0)
+
+        x_tiles = {}
+        w_tiles = {}
+
+        def load_x(r):
+            stream = streams[r // STREAM_ROUNDS]
+            first = (r % STREAM_ROUNDS) * ROUND_K
+            x_sb = x_pool.tile([P, EDGE_TILES, ROUND_K], BF16)
+            nc.sync.dma_start(
+                out=x_sb[:],
+                in_=stream[:, first : first + ROUND_K].rearrange("(m p) c -> p m c", p=P),
+            )
+            x_tiles[r] = x_sb
+
+        def load_weight(first_group):
+            w_sb = weights.tile(
+                [P, ROUND_GROUPS, LATENT], U32, name="w%d" % first_group, align_bytes=64
+            )
+            nc.sync.dma_start(
+                out=w_sb[:].bitcast(I32),
+                in_=W1_words[first_group : first_group + ROUND_GROUPS]
+                .rearrange("g p n t -> p g (n t)")
+                .bitcast(I32),
+            )
+            w_tiles[first_group] = w_sb
+
+        def load_scales():
+            scale_words = W1_scales.bitcast(I32)
+            for quadrant in range(4):
+                for row in range(4):
+                    first = 32 * quadrant + row
+                    nc.sync.dma_start(
+                        out=w_planes[first : first + 4 * PLANES_PER_TILE : 4, :, :].bitcast(I32),
+                        in_=scale_words[:, 4 * quadrant + row, :].rearrange(
+                            "(s o) n -> o s n", o=PLANES_PER_TILE
+                        ),
+                    )
+
+        def w_plane(group):
+            return w_planes[4 * (group % PLANES_PER_TILE) : P, group // PLANES_PER_TILE, :]
+
+        def load_round(r):
+            if r < ROUNDS:
+                load_weight(ROUND_GROUPS * r)
+            if GLOB_LOAD_ROUND <= r < GLOB_LOAD_ROUND + STREAM_ROUNDS:
+                load_weight(X_GROUPS + ROUND_GROUPS * (r - GLOB_LOAD_ROUND))
+            if r + 2 < ROUNDS:
+                load_x(r + 2)
+
+        load_x(0)
+        load_x(1)
+        nc.sync.dma_start(out=b_rows[0:1, :], in_=b1.unsqueeze(0))
+        glob_sb = const.tile([P, STREAM_GROUPS, PACK], BF16)
+        nc.sync.dma_start(
+            out=glob_sb[:],
+            in_=global_attr.rearrange("o (g p t) -> p (o g) t", p=P, t=PACK),
+        )
+        load_scales()
+        for r in range(X_AHEAD - 2):
+            load_round(r)
+
+        def quantise_round(r):
+            x_words = x_tiles[r][:].bitcast(F32)
+            banks = []
+            for m in range(EDGE_TILES):
+                bank = bank_pool.tile([P, ROUND_GROUPS, 2, P], F32, name="bank")
+                for g in range(ROUND_GROUPS):
+                    for u in range(2):
+                        nc.tensor.transpose(
+                            bank[:, g, u, :],
+                            x_words[:, m, g * GROUP_WORDS + u : (g + 1) * GROUP_WORDS : 2],
+                            identity[:],
+                        )
+                banks.append(bank)
+
+            grouped = grouped_pool.tile([P, EDGE_TILES, ROUND_K], BF16, align_bytes=64)
+            for m in range(EDGE_TILES):
+                copy = nc.scalar.copy if m % 2 == 0 else nc.vector.tensor_copy
+                copy(
+                    out=grouped[:, m, :]
+                    .bitcast(F32)
+                    .rearrange("p (g e u) -> p g e u", g=ROUND_GROUPS, u=2),
+                    in_=banks[m][:].rearrange("p g u e -> p g e u"),
+                )
+
+            codes = quantised_pool.tile([P, EDGE_TILES, ROUND_GROUPS, P], U32, align_bytes=64)
+            planes = quantised_pool.tile([P, EDGE_TILES, ROUND_GROUPS, P], U8, align_bytes=64)
+            for m in range(0, EDGE_TILES, 2):
+                nc.vector.quantize_mx(
+                    out=codes[:, m : m + 2].rearrange("p m g e -> p (m g e)").bitcast(FP8X4),
+                    scales=planes[:, m : m + 2].rearrange("p m g e -> p (m g e)"),
+                    in_=grouped[:, m : m + 2, :].rearrange("p m c -> p (m c)"),
+                )
+            return codes, planes
+
+        sums = [
+            sums_pool.tile([P, LATENT], F32, name="sum%d" % m) for m in range(EDGE_TILES)
+        ]
+
+        def multiply_tile(r, m, codes, planes):
+            for g in range(ROUND_GROUPS):
+                group = ROUND_GROUPS * r + g
+                nc.tensor.matmul_mx(
+                    out=sums[m][:],
+                    lhsT=codes[:, m, g, :].bitcast(FP8X4),
+                    lhsT_scale=planes[:, m, g, :],
+                    rhs=w_tiles[ROUND_GROUPS * r][:, g, :].bitcast(FP8X4),
+                    rhs_scale=w_plane(group),
+                    start=(group == 0),
+                    stop=(group == X_GROUPS - 1),
+                )
+
+        quantised = {0: quantise_round(0)}
+
+        b_bank = bank_pool.tile([P, LATENT], F32, name="b_bank", tag="bank")
+        nc.tensor.matmul(out=b_bank[:], lhsT=ones[:], rhs=b_rows[:], start=True, stop=True)
+        b_all = const.tile([P, LATENT], F32)
+        nc.scalar.copy(out=b_all[:], in_=b_bank[:])
+
+        glob_grouped = const.tile([P, STREAM_GROUPS, P, PACK], BF16, align_bytes=64)
+        nc.vector.tensor_copy(
+            out=glob_grouped[:],
+            in_=glob_sb[:].unsqueeze(2).to_broadcast([P, STREAM_GROUPS, P, PACK]),
+        )
+        glob_codes = const.tile([P, STREAM_GROUPS, P], U32, align_bytes=64)
+        glob_planes = const.tile([P, STREAM_GROUPS, P], U8, align_bytes=64)
+        nc.vector.quantize_mx(
+            out=glob_codes[:].rearrange("p g e -> p (g e)").bitcast(FP8X4),
+            scales=glob_planes[:].rearrange("p g e -> p (g e)"),
+            in_=glob_grouped[:].rearrange("p g e t -> p (g e t)"),
+        )
+        shared_row = const.tile([P, LATENT], F32)
+
+        for r in range(ROUNDS):
+            load_round(r + X_AHEAD - 2)
+            if r + 1 < ROUNDS:
+                quantised[r + 1] = quantise_round(r + 1)
+            codes, planes = quantised[r]
+            for m in range(EDGE_TILES):
+                multiply_tile(r, m, codes, planes)
+                if r == ROUNDS - 1:
+                    summed = result_pool.tile([P, LATENT], F32)
+                    nc.vector.tensor_tensor(
+                        out=summed[:], in0=sums[m][:], in1=shared_row[:], op=mybir.AluOpType.add
+                    )
+                    result = result_pool.tile([P, LATENT], F32)
+                    nc.scalar.activation(
+                        out=result[:], in_=summed[:], func=mybir.ActivationFunctionType.Relu
+                    )
+                    nc.sync.dma_start(out=out[m * P : (m + 1) * P, :], in_=result[:])
+
+            if r == GLOB_ROUND:
+                glob_bank = bank_pool.tile([P, LATENT], F32, name="glob_bank", tag="bank")
+                for g in range(STREAM_GROUPS):
+                    group = X_GROUPS + g
+                    nc.tensor.matmul_mx(
+                        out=glob_bank[:],
+                        lhsT=glob_codes[:, g, :].bitcast(FP8X4),
+                        lhsT_scale=glob_planes[:, g, :],
+                        rhs=w_tiles[group - group % ROUND_GROUPS][:, group % ROUND_GROUPS, :].bitcast(FP8X4),
+                        rhs_scale=w_plane(group),
+                        start=(g == 0),
+                        stop=(g == STREAM_GROUPS - 1),
+                    )
+                nc.vector.tensor_tensor(
+                    out=shared_row[:], in0=glob_bank[:], in1=b_all[:], op=mybir.AluOpType.add
+                )

@@ -13,7 +13,6 @@ FP8X4 = mybir.dt.float8_e4m3fn_x4
 P = 128
 PACK = 4
 GROUP_K = P * PACK
-GROUP_WORDS = GROUP_K // 2
 EDGES = 512
 EDGE_TILES = EDGES // P
 D_STREAM = 4096
@@ -24,7 +23,7 @@ ROUND_GROUPS = 2
 ROUND_K = ROUND_GROUPS * GROUP_K
 ROUNDS = X_GROUPS // ROUND_GROUPS
 STREAM_ROUNDS = STREAM_GROUPS // ROUND_GROUPS
-X_AHEAD = 5
+X_BUFS = 6
 PLANES_PER_TILE = 4
 GLOB_LOAD_ROUND = 5
 GLOB_ROUND = 9
@@ -41,7 +40,8 @@ def tile_edgemodel_pa_k_kernel(
     with ExitStack() as ctx:
         const = ctx.enter_context(tc.tile_pool(name="const", bufs=1))
         weights = ctx.enter_context(tc.tile_pool(name="weights", bufs=1))
-        x_pool = ctx.enter_context(tc.tile_pool(name="x", bufs=X_AHEAD + 1))
+        x_pool = ctx.enter_context(tc.tile_pool(name="x", bufs=X_BUFS))
+        sorted_pool = ctx.enter_context(tc.tile_pool(name="sorted", bufs=2))
         grouped_pool = ctx.enter_context(tc.tile_pool(name="grouped", bufs=2))
         quantised_pool = ctx.enter_context(tc.tile_pool(name="quantised", bufs=3))
         result_pool = ctx.enter_context(tc.tile_pool(name="result", bufs=2))
@@ -115,11 +115,23 @@ def tile_edgemodel_pa_k_kernel(
             in_=global_attr.rearrange("o (g p t) -> p (o g) t", p=P, t=PACK),
         )
         load_scales()
-        for r in range(X_AHEAD - 2):
+        for r in range(X_BUFS - 2):
             load_round(r)
 
+        sorted_tiles = {}
+
+        def sort_round(r):
+            sorted_words = sorted_pool.tile([P, EDGE_TILES * ROUND_GROUPS, 2, P], F32)
+            nc.vector.tensor_copy(
+                out=sorted_words[:],
+                in_=x_tiles[r][:]
+                .bitcast(F32)
+                .rearrange("p m (g j u) -> p (m g) u j", g=ROUND_GROUPS, u=2),
+            )
+            sorted_tiles[r] = sorted_words
+
         def quantise_round(r):
-            x_words = x_tiles[r][:].bitcast(F32)
+            sorted_words = sorted_tiles[r]
             banks = []
             for m in range(EDGE_TILES):
                 bank = bank_pool.tile([P, ROUND_GROUPS, 2, P], F32, name="bank")
@@ -127,15 +139,14 @@ def tile_edgemodel_pa_k_kernel(
                     for u in range(2):
                         nc.tensor.transpose(
                             bank[:, g, u, :],
-                            x_words[:, m, g * GROUP_WORDS + u : (g + 1) * GROUP_WORDS : 2],
+                            sorted_words[:, m * ROUND_GROUPS + g, u, :],
                             identity[:],
                         )
                 banks.append(bank)
 
             grouped = grouped_pool.tile([P, EDGE_TILES, ROUND_K], BF16, align_bytes=64)
             for m in range(EDGE_TILES):
-                copy = nc.scalar.copy if m % 2 == 0 else nc.vector.tensor_copy
-                copy(
+                nc.scalar.copy(
                     out=grouped[:, m, :]
                     .bitcast(F32)
                     .rearrange("p (g e u) -> p g e u", g=ROUND_GROUPS, u=2),
@@ -169,6 +180,8 @@ def tile_edgemodel_pa_k_kernel(
                     stop=(group == X_GROUPS - 1),
                 )
 
+        sort_round(0)
+        sort_round(1)
         quantised = {0: quantise_round(0)}
 
         b_bank = bank_pool.tile([P, LATENT], F32, name="b_bank", tag="bank")
@@ -191,7 +204,9 @@ def tile_edgemodel_pa_k_kernel(
         shared_row = const.tile([P, LATENT], F32)
 
         for r in range(ROUNDS):
-            load_round(r + X_AHEAD - 2)
+            load_round(r + X_BUFS - 2)
+            if r + 2 < ROUNDS:
+                sort_round(r + 2)
             if r + 1 < ROUNDS:
                 quantised[r + 1] = quantise_round(r + 1)
             codes, planes = quantised[r]

@@ -22,6 +22,7 @@ X_GROUPS = 3 * STREAM_GROUPS
 ROUND_GROUPS = 2
 ROUND_K = ROUND_GROUPS * GROUP_K
 ROUNDS = X_GROUPS // ROUND_GROUPS
+ROUNDS_PER_SET = 2
 STREAM_ROUNDS = STREAM_GROUPS // ROUND_GROUPS
 X_BUFS = 6
 PLANES_PER_TILE = 4
@@ -57,6 +58,8 @@ def tile_edgemodel_pa_k_kernel(
         nc.vector.memset(w_planes[:].bitcast(I32), 0)
         b_rows = const.tile([P, LATENT], BF16)
         nc.vector.memset(b_rows[:].bitcast(I32), 0)
+        glob_rows = const.tile([P, GROUP_K], BF16)
+        nc.vector.memset(glob_rows[:].bitcast(I32), 0)
 
         x_tiles = {}
         w_tiles = {}
@@ -65,10 +68,14 @@ def tile_edgemodel_pa_k_kernel(
             stream = streams[r // STREAM_ROUNDS]
             first = (r % STREAM_ROUNDS) * ROUND_K
             x_sb = x_pool.tile([P, EDGE_TILES, ROUND_K], BF16)
-            nc.sync.dma_start(
-                out=x_sb[:],
-                in_=stream[:, first : first + ROUND_K].rearrange("(m p) c -> p m c", p=P),
-            )
+            tiles = 1 if r == 0 else EDGE_TILES
+            for m in range(0, EDGE_TILES, tiles):
+                nc.sync.dma_start(
+                    out=x_sb[:, m : m + tiles, :],
+                    in_=stream[m * P : (m + tiles) * P, first : first + ROUND_K].rearrange(
+                        "(m p) c -> p m c", p=P
+                    ),
+                )
             x_tiles[r] = x_sb
 
         def load_weight(first_group):
@@ -83,51 +90,57 @@ def tile_edgemodel_pa_k_kernel(
             )
             w_tiles[first_group] = w_sb
 
-        def load_scales():
-            scale_words = W1_scales.bitcast(I32)
+        scale_words = W1_scales.bitcast(I32)
+
+        def load_scales(s):
             for quadrant in range(4):
-                for row in range(4):
-                    first = 32 * quadrant + row
-                    nc.sync.dma_start(
-                        out=w_planes[first : first + 4 * PLANES_PER_TILE : 4, :, :].bitcast(I32),
-                        in_=scale_words[:, 4 * quadrant + row, :].rearrange(
-                            "(s o) n -> o s n", o=PLANES_PER_TILE
-                        ),
-                    )
+                nc.sync.dma_start(
+                    out=w_planes[32 * quadrant : 32 * quadrant + 16, s, :].bitcast(I32),
+                    in_=scale_words[
+                        PLANES_PER_TILE * s : PLANES_PER_TILE * (s + 1),
+                        4 * quadrant : 4 * quadrant + 4,
+                        :,
+                    ],
+                )
 
         def w_plane(group):
             return w_planes[4 * (group % PLANES_PER_TILE) : P, group // PLANES_PER_TILE, :]
 
         def load_round(r):
             if r < ROUNDS:
+                if r % ROUNDS_PER_SET == 0:
+                    load_scales(r // ROUNDS_PER_SET)
                 load_weight(ROUND_GROUPS * r)
             if GLOB_LOAD_ROUND <= r < GLOB_LOAD_ROUND + STREAM_ROUNDS:
-                load_weight(X_GROUPS + ROUND_GROUPS * (r - GLOB_LOAD_ROUND))
-            if r + 2 < ROUNDS:
-                load_x(r + 2)
+                piece = r - GLOB_LOAD_ROUND
+                if piece % ROUNDS_PER_SET == 0:
+                    load_scales((ROUNDS + piece) // ROUNDS_PER_SET)
+                load_weight(X_GROUPS + ROUND_GROUPS * piece)
+            if r + 1 < ROUNDS:
+                load_x(r + 1)
 
         load_x(0)
-        load_x(1)
-        nc.sync.dma_start(out=b_rows[0:1, :], in_=b1.unsqueeze(0))
-        glob_sb = const.tile([P, STREAM_GROUPS, PACK], BF16)
+        load_round(0)
         nc.sync.dma_start(
-            out=glob_sb[:],
-            in_=global_attr.rearrange("o (g p t) -> p (o g) t", p=P, t=PACK),
+            out=glob_rows[0:STREAM_GROUPS, :],
+            in_=global_attr.rearrange("o (g c) -> (o g) c", g=STREAM_GROUPS),
         )
-        load_scales()
-        for r in range(X_BUFS - 2):
+        nc.sync.dma_start(out=b_rows[0:1, :], in_=b1.unsqueeze(0))
+        for r in range(1, X_BUFS - 1):
             load_round(r)
 
         sorted_tiles = {}
 
         def sort_round(r):
             sorted_words = sorted_pool.tile([P, EDGE_TILES * ROUND_GROUPS, 2, P], F32)
-            nc.vector.tensor_copy(
-                out=sorted_words[:],
-                in_=x_tiles[r][:]
-                .bitcast(F32)
-                .rearrange("p m (g j u) -> p (m g) u j", g=ROUND_GROUPS, u=2),
-            )
+            tiles = 1 if r == 0 else EDGE_TILES
+            for m in range(0, EDGE_TILES, tiles):
+                nc.vector.tensor_copy(
+                    out=sorted_words[:, m * ROUND_GROUPS : (m + tiles) * ROUND_GROUPS],
+                    in_=x_tiles[r][:, m : m + tiles, :]
+                    .bitcast(F32)
+                    .rearrange("p m (g j u) -> p (m g) u j", g=ROUND_GROUPS, u=2),
+                )
             sorted_tiles[r] = sorted_words
 
         def quantise_round(r):
@@ -181,13 +194,24 @@ def tile_edgemodel_pa_k_kernel(
                 )
 
         sort_round(0)
-        sort_round(1)
         quantised = {0: quantise_round(0)}
+        sort_round(1)
 
         b_bank = bank_pool.tile([P, LATENT], F32, name="b_bank", tag="bank")
         nc.tensor.matmul(out=b_bank[:], lhsT=ones[:], rhs=b_rows[:], start=True, stop=True)
         b_all = const.tile([P, LATENT], F32)
         nc.scalar.copy(out=b_all[:], in_=b_bank[:])
+
+        glob_bank = bank_pool.tile([P, 2, P], F32, name="glob_t_bank", tag="bank")
+        for u in range(2):
+            nc.tensor.transpose(
+                glob_bank[:, u, :], glob_rows[:].bitcast(F32)[:, u::2], identity[:]
+            )
+        glob_sb = const.tile([P, STREAM_GROUPS, PACK], BF16)
+        nc.scalar.copy(
+            out=glob_sb[:].rearrange("p g t -> p (g t)").bitcast(F32).rearrange("p (g u) -> p g u", u=2),
+            in_=glob_bank[:, :, 0:STREAM_GROUPS].rearrange("p u g -> p g u"),
+        )
 
         glob_grouped = const.tile([P, STREAM_GROUPS, P, PACK], BF16, align_bytes=64)
         nc.vector.tensor_copy(
@@ -204,7 +228,7 @@ def tile_edgemodel_pa_k_kernel(
         shared_row = const.tile([P, LATENT], F32)
 
         for r in range(ROUNDS):
-            load_round(r + X_BUFS - 2)
+            load_round(r + X_BUFS - 1)
             if r + 2 < ROUNDS:
                 sort_round(r + 2)
             if r + 1 < ROUNDS:

@@ -17,17 +17,17 @@ EDGES = 512
 EDGE_TILES = EDGES // P
 D_STREAM = 4096
 LATENT = 512
+HALF = LATENT // 2
 STREAM_GROUPS = D_STREAM // GROUP_K
 X_GROUPS = 3 * STREAM_GROUPS
-ROUND_GROUPS = 2
-ROUND_K = ROUND_GROUPS * GROUP_K
-ROUNDS = X_GROUPS // ROUND_GROUPS
-ROUNDS_PER_SET = 2
-STREAM_ROUNDS = STREAM_GROUPS // ROUND_GROUPS
+W_GROUPS = 2
+LAST_GROUPS = (X_GROUPS - 2, X_GROUPS - 1)
+PAIRS = 8
+BANK_PAIRS = 2
 X_BUFS = 6
-PLANES_PER_TILE = 4
-GLOB_LOAD_ROUND = 5
-GLOB_ROUND = 9
+FIRST_LAST_CHUNK = 8
+GLOB_CHUNK = 10
+PLANES_PER_SET = 4
 
 FLOPS = 2 * EDGES * (4 * D_STREAM) * LATENT
 
@@ -38,24 +38,27 @@ def tile_edgemodel_pa_k_kernel(
     nc = tc.nc
     streams = (receiver, sender, edge_attr)
 
+    chunks = [(0, m, 2, g, 4) for g in (0, 4) for m in (0, 2)]
+    chunks += [(s, m, 1, 0, STREAM_GROUPS) for s in (1, 2) for m in range(EDGE_TILES)]
+
     with ExitStack() as ctx:
         const = ctx.enter_context(tc.tile_pool(name="const", bufs=1))
         weights = ctx.enter_context(tc.tile_pool(name="weights", bufs=1))
         x_pool = ctx.enter_context(tc.tile_pool(name="x", bufs=X_BUFS))
         sorted_pool = ctx.enter_context(tc.tile_pool(name="sorted", bufs=2))
         grouped_pool = ctx.enter_context(tc.tile_pool(name="grouped", bufs=2))
-        quantised_pool = ctx.enter_context(tc.tile_pool(name="quantised", bufs=3))
-        result_pool = ctx.enter_context(tc.tile_pool(name="result", bufs=2))
+        quantised_pool = ctx.enter_context(tc.tile_pool(name="quantised", bufs=6))
+        result_pool = ctx.enter_context(tc.tile_pool(name="result", bufs=4))
         sums_pool = ctx.enter_context(tc.psum_pool(name="sums", bufs=1))
         bank_pool = ctx.enter_context(tc.psum_pool(name="bank", bufs=4))
         ctx.enter_context(tc.manual_schedule())
 
         identity = const.tile([P, P], F32)
         make_identity(nc, identity[:])
+        w_planes = const.tile([P, 4 * STREAM_GROUPS // PLANES_PER_SET, LATENT], U8, align_bytes=64)
+        nc.vector.memset(w_planes[:].bitcast(I32), 0)
         ones = const.tile([P, P], BF16)
         nc.vector.memset(ones[:], 1.0)
-        w_planes = const.tile([P, 4 * STREAM_GROUPS // PLANES_PER_TILE, LATENT], U8, align_bytes=64)
-        nc.vector.memset(w_planes[:].bitcast(I32), 0)
         b_rows = const.tile([P, LATENT], BF16)
         nc.vector.memset(b_rows[:].bitcast(I32), 0)
         glob_rows = const.tile([P, GROUP_K], BF16)
@@ -64,31 +67,31 @@ def tile_edgemodel_pa_k_kernel(
         x_tiles = {}
         w_tiles = {}
 
-        def load_x(r):
-            stream = streams[r // STREAM_ROUNDS]
-            first = (r % STREAM_ROUNDS) * ROUND_K
-            x_sb = x_pool.tile([P, EDGE_TILES, ROUND_K], BF16)
-            tiles = 1 if r == 0 else EDGE_TILES
-            for m in range(0, EDGE_TILES, tiles):
+        def load_x(c, pieces=1):
+            s, m, tiles, g, groups = chunks[c]
+            x_sb = x_pool.tile([P, tiles, groups * GROUP_K], BF16)
+            step = tiles // pieces
+            for i in range(0, tiles, step):
                 nc.sync.dma_start(
-                    out=x_sb[:, m : m + tiles, :],
-                    in_=stream[m * P : (m + tiles) * P, first : first + ROUND_K].rearrange(
-                        "(m p) c -> p m c", p=P
-                    ),
+                    out=x_sb[:, i : i + step, :],
+                    in_=streams[s][
+                        (m + i) * P : (m + i + step) * P, g * GROUP_K : (g + groups) * GROUP_K
+                    ].rearrange("(m p) c -> p m c", p=P),
                 )
-            x_tiles[r] = x_sb
+            x_tiles[c] = x_sb
 
-        def load_weight(first_group):
+        def load_weight(first_group, column=0, columns=LATENT):
             w_sb = weights.tile(
-                [P, ROUND_GROUPS, LATENT], U32, name="w%d" % first_group, align_bytes=64
+                [P, W_GROUPS, columns], U32, name="w%d_%d" % (first_group, column), align_bytes=64
             )
             nc.sync.dma_start(
                 out=w_sb[:].bitcast(I32),
-                in_=W1_words[first_group : first_group + ROUND_GROUPS]
+                in_=W1_words[first_group : first_group + W_GROUPS, :, column : column + columns, :]
                 .rearrange("g p n t -> p g (n t)")
                 .bitcast(I32),
             )
-            w_tiles[first_group] = w_sb
+            for g in range(W_GROUPS):
+                w_tiles[first_group + g, column] = w_sb[:, g, :]
 
         scale_words = W1_scales.bitcast(I32)
 
@@ -97,169 +100,240 @@ def tile_edgemodel_pa_k_kernel(
                 nc.sync.dma_start(
                     out=w_planes[32 * quadrant : 32 * quadrant + 16, s, :].bitcast(I32),
                     in_=scale_words[
-                        PLANES_PER_TILE * s : PLANES_PER_TILE * (s + 1),
+                        PLANES_PER_SET * s : PLANES_PER_SET * (s + 1),
                         4 * quadrant : 4 * quadrant + 4,
                         :,
                     ],
                 )
 
-        def w_plane(group):
-            return w_planes[4 * (group % PLANES_PER_TILE) : P, group // PLANES_PER_TILE, :]
+        def w_plane(group, column=0, columns=LATENT):
+            return w_planes[
+                4 * (group % PLANES_PER_SET) : P,
+                group // PLANES_PER_SET,
+                column : column + columns,
+            ]
 
-        def load_round(r):
-            if r < ROUNDS:
-                if r % ROUNDS_PER_SET == 0:
-                    load_scales(r // ROUNDS_PER_SET)
-                load_weight(ROUND_GROUPS * r)
-            if GLOB_LOAD_ROUND <= r < GLOB_LOAD_ROUND + STREAM_ROUNDS:
-                piece = r - GLOB_LOAD_ROUND
-                if piece % ROUNDS_PER_SET == 0:
-                    load_scales((ROUNDS + piece) // ROUNDS_PER_SET)
-                load_weight(X_GROUPS + ROUND_GROUPS * piece)
-            if r + 1 < ROUNDS:
-                load_x(r + 1)
-
-        load_x(0)
-        load_round(0)
+        load_x(0, pieces=2)
+        load_scales(0)
+        load_weight(0)
+        load_weight(2)
+        load_x(1)
         nc.sync.dma_start(
             out=glob_rows[0:STREAM_GROUPS, :],
             in_=global_attr.rearrange("o (g c) -> (o g) c", g=STREAM_GROUPS),
         )
         nc.sync.dma_start(out=b_rows[0:1, :], in_=b1.unsqueeze(0))
-        for r in range(1, X_BUFS - 1):
-            load_round(r)
+        load_x(2)
+        load_scales(1)
+        load_weight(4)
+        load_weight(6)
+        load_x(3)
+        load_x(4)
+        load_scales(2)
+        load_weight(8)
+        load_weight(10)
+        load_scales(3)
+        load_weight(12)
+        load_weight(14)
+
+        def load_ahead(c):
+            if 5 <= c < len(chunks):
+                load_x(c)
+            if c == 8:
+                load_scales(4)
+                load_weight(16)
+                load_weight(18)
+                load_scales(5)
+                load_weight(20)
+            if c == len(chunks) - 1:
+                load_scales(6)
+                load_weight(24)
+                load_weight(26)
+                load_scales(7)
+                load_weight(28)
+                load_weight(30)
+                load_weight(LAST_GROUPS[0], 0, HALF)
+                load_weight(LAST_GROUPS[0], HALF, HALF)
 
         sorted_tiles = {}
+        quantised = {}
 
-        def sort_round(r):
-            sorted_words = sorted_pool.tile([P, EDGE_TILES * ROUND_GROUPS, 2, P], F32)
-            tiles = 1 if r == 0 else EDGE_TILES
-            for m in range(0, EDGE_TILES, tiles):
-                nc.vector.tensor_copy(
-                    out=sorted_words[:, m * ROUND_GROUPS : (m + tiles) * ROUND_GROUPS],
-                    in_=x_tiles[r][:, m : m + tiles, :]
-                    .bitcast(F32)
-                    .rearrange("p m (g j u) -> p (m g) u j", g=ROUND_GROUPS, u=2),
-                )
-            sorted_tiles[r] = sorted_words
+        def sort_half(c, half):
+            if half == 0:
+                sorted_words = sorted_pool.tile([P, PAIRS, 2, P], F32)
+                sorted_tiles[c] = sorted_words
+            first = half * PAIRS // 2
+            x_words = x_tiles[c][:].rearrange("p m c -> p (m c)").bitcast(F32)
+            nc.vector.tensor_copy(
+                out=sorted_tiles[c][:, first : first + PAIRS // 2],
+                in_=x_words[:, first * 2 * P : (first + PAIRS // 2) * 2 * P].rearrange(
+                    "p (i j u) -> p i u j", i=PAIRS // 2, u=2
+                ),
+            )
 
-        def quantise_round(r):
-            sorted_words = sorted_tiles[r]
+        def transpose_chunk(c):
+            grouped = grouped_pool.tile([P, PAIRS, P * PACK], BF16, align_bytes=64)
             banks = []
-            for m in range(EDGE_TILES):
-                bank = bank_pool.tile([P, ROUND_GROUPS, 2, P], F32, name="bank")
-                for g in range(ROUND_GROUPS):
+            for first in range(0, PAIRS, BANK_PAIRS):
+                bank = bank_pool.tile([P, BANK_PAIRS, 2, P], F32, name="bank")
+                for i in range(BANK_PAIRS):
                     for u in range(2):
                         nc.tensor.transpose(
-                            bank[:, g, u, :],
-                            sorted_words[:, m * ROUND_GROUPS + g, u, :],
-                            identity[:],
+                            bank[:, i, u, :], sorted_tiles[c][:, first + i, u, :], identity[:]
                         )
                 banks.append(bank)
-
-            grouped = grouped_pool.tile([P, EDGE_TILES, ROUND_K], BF16, align_bytes=64)
-            for m in range(EDGE_TILES):
+            for i, bank in enumerate(banks):
                 nc.scalar.copy(
-                    out=grouped[:, m, :]
+                    out=grouped[:, BANK_PAIRS * i : BANK_PAIRS * (i + 1), :]
+                    .rearrange("p i c -> p (i c)")
                     .bitcast(F32)
-                    .rearrange("p (g e u) -> p g e u", g=ROUND_GROUPS, u=2),
-                    in_=banks[m][:].rearrange("p g u e -> p g e u"),
+                    .rearrange("p (i e u) -> p i e u", i=BANK_PAIRS, u=2),
+                    in_=bank[:].rearrange("p i u e -> p i e u"),
                 )
+            codes = quantised_pool.tile([P, PAIRS, P], U32, align_bytes=64)
+            planes = quantised_pool.tile([P, PAIRS, P], U8, align_bytes=64)
+            quantised[c] = (grouped, codes, planes)
 
-            codes = quantised_pool.tile([P, EDGE_TILES, ROUND_GROUPS, P], U32, align_bytes=64)
-            planes = quantised_pool.tile([P, EDGE_TILES, ROUND_GROUPS, P], U8, align_bytes=64)
-            for m in range(0, EDGE_TILES, 2):
-                nc.vector.quantize_mx(
-                    out=codes[:, m : m + 2].rearrange("p m g e -> p (m g e)").bitcast(FP8X4),
-                    scales=planes[:, m : m + 2].rearrange("p m g e -> p (m g e)"),
-                    in_=grouped[:, m : m + 2, :].rearrange("p m c -> p (m c)"),
-                )
-            return codes, planes
+        def quantise_half(c, half):
+            grouped, codes, planes = quantised[c]
+            part = slice(half * PAIRS // 2, (half + 1) * PAIRS // 2)
+            nc.vector.quantize_mx(
+                out=codes[:, part].rearrange("p i e -> p (i e)").bitcast(FP8X4),
+                scales=planes[:, part].rearrange("p i e -> p (i e)"),
+                in_=grouped[:, part, :].rearrange("p i c -> p (i c)"),
+            )
 
         sums = [
             sums_pool.tile([P, LATENT], F32, name="sum%d" % m) for m in range(EDGE_TILES)
         ]
+        last_codes = {}
 
-        def multiply_tile(r, m, codes, planes):
-            for g in range(ROUND_GROUPS):
-                group = ROUND_GROUPS * r + g
+        def multiply_chunk(c):
+            s, m, tiles, g, groups = chunks[c]
+            codes, planes = quantised[c][1:]
+            for pair in range(PAIRS):
+                tile = m + pair // groups
+                group = STREAM_GROUPS * s + g + pair % groups
+                if group in LAST_GROUPS:
+                    last_codes[tile, group] = (codes[:, pair, :], planes[:, pair, :])
+                    continue
                 nc.tensor.matmul_mx(
-                    out=sums[m][:],
-                    lhsT=codes[:, m, g, :].bitcast(FP8X4),
-                    lhsT_scale=planes[:, m, g, :],
-                    rhs=w_tiles[ROUND_GROUPS * r][:, g, :].bitcast(FP8X4),
+                    out=sums[tile][:],
+                    lhsT=codes[:, pair, :].bitcast(FP8X4),
+                    lhsT_scale=planes[:, pair, :],
+                    rhs=w_tiles[group, 0].bitcast(FP8X4),
                     rhs_scale=w_plane(group),
                     start=(group == 0),
-                    stop=(group == X_GROUPS - 1),
+                    stop=(group == LAST_GROUPS[0] - 1),
                 )
 
-        sort_round(0)
-        quantised = {0: quantise_round(0)}
-        sort_round(1)
+        def multiply_glob():
+            shared_bank = bank_pool.tile([P, LATENT], F32, name="shared_bank", tag="bank")
+            for g in range(STREAM_GROUPS):
+                nc.tensor.matmul_mx(
+                    out=shared_bank[:],
+                    lhsT=glob_codes[:, g, :].bitcast(FP8X4),
+                    lhsT_scale=glob_planes[:, g, :],
+                    rhs=w_tiles[X_GROUPS + g, 0].bitcast(FP8X4),
+                    rhs_scale=w_plane(X_GROUPS + g),
+                    start=(g == 0),
+                    stop=(g == STREAM_GROUPS - 1),
+                )
+            nc.vector.tensor_tensor(
+                out=shared_row[:], in0=shared_bank[:], in1=b_all[:], op=mybir.AluOpType.add
+            )
+
+        partials = []
+
+        def bias_tile(m):
+            partial = const.tile([P, LATENT], F32, name="partial%d" % m)
+            nc.vector.tensor_tensor(
+                out=partial[:], in0=sums[m][:], in1=shared_row[:], op=mybir.AluOpType.add
+            )
+            partials.append(partial)
+
+        sort_half(0, 0)
+        sort_half(0, 1)
+        transpose_chunk(0)
+        quantise_half(0, 0)
+        quantise_half(0, 1)
+        multiply_chunk(0)
+        sort_half(1, 0)
+        sort_half(1, 1)
 
         b_bank = bank_pool.tile([P, LATENT], F32, name="b_bank", tag="bank")
         nc.tensor.matmul(out=b_bank[:], lhsT=ones[:], rhs=b_rows[:], start=True, stop=True)
-        b_all = const.tile([P, LATENT], F32)
-        nc.scalar.copy(out=b_all[:], in_=b_bank[:])
-
-        glob_bank = bank_pool.tile([P, 2, P], F32, name="glob_t_bank", tag="bank")
+        glob_bank = bank_pool.tile([P, 2, P], F32, name="glob_bank", tag="bank")
         for u in range(2):
             nc.tensor.transpose(
                 glob_bank[:, u, :], glob_rows[:].bitcast(F32)[:, u::2], identity[:]
             )
+        b_all = const.tile([P, LATENT], F32)
+        nc.scalar.copy(out=b_all[:], in_=b_bank[:])
         glob_sb = const.tile([P, STREAM_GROUPS, PACK], BF16)
         nc.scalar.copy(
             out=glob_sb[:].rearrange("p g t -> p (g t)").bitcast(F32).rearrange("p (g u) -> p g u", u=2),
             in_=glob_bank[:, :, 0:STREAM_GROUPS].rearrange("p u g -> p g u"),
         )
-
+        transpose_chunk(1)
         glob_grouped = const.tile([P, STREAM_GROUPS, P, PACK], BF16, align_bytes=64)
-        nc.vector.tensor_copy(
-            out=glob_grouped[:],
-            in_=glob_sb[:].unsqueeze(2).to_broadcast([P, STREAM_GROUPS, P, PACK]),
-        )
         glob_codes = const.tile([P, STREAM_GROUPS, P], U32, align_bytes=64)
         glob_planes = const.tile([P, STREAM_GROUPS, P], U8, align_bytes=64)
-        nc.vector.quantize_mx(
-            out=glob_codes[:].rearrange("p g e -> p (g e)").bitcast(FP8X4),
-            scales=glob_planes[:].rearrange("p g e -> p (g e)"),
-            in_=glob_grouped[:].rearrange("p g e t -> p (g e t)"),
-        )
         shared_row = const.tile([P, LATENT], F32)
 
-        for r in range(ROUNDS):
-            load_round(r + X_BUFS - 1)
-            if r + 2 < ROUNDS:
-                sort_round(r + 2)
-            if r + 1 < ROUNDS:
-                quantised[r + 1] = quantise_round(r + 1)
-            codes, planes = quantised[r]
-            for m in range(EDGE_TILES):
-                multiply_tile(r, m, codes, planes)
-                if r == ROUNDS - 1:
-                    summed = result_pool.tile([P, LATENT], F32)
-                    nc.vector.tensor_tensor(
-                        out=summed[:], in0=sums[m][:], in1=shared_row[:], op=mybir.AluOpType.add
-                    )
-                    result = result_pool.tile([P, LATENT], F32)
-                    nc.scalar.activation(
-                        out=result[:], in_=summed[:], func=mybir.ActivationFunctionType.Relu
-                    )
-                    nc.sync.dma_start(out=out[m * P : (m + 1) * P, :], in_=result[:])
+        for c in range(1, len(chunks)):
+            load_ahead(c + 4)
+            if c + 1 < len(chunks):
+                sort_half(c + 1, 0)
+                sort_half(c + 1, 1)
+            quantise_half(c, 0)
+            quantise_half(c, 1)
+            if c + 1 < len(chunks):
+                transpose_chunk(c + 1)
+            if c == 3:
+                nc.vector.tensor_copy(
+                    out=glob_grouped[:],
+                    in_=glob_sb[:].unsqueeze(2).to_broadcast([P, STREAM_GROUPS, P, PACK]),
+                )
+            if c == 4:
+                nc.vector.quantize_mx(
+                    out=glob_codes[:].rearrange("p g e -> p (g e)").bitcast(FP8X4),
+                    scales=glob_planes[:].rearrange("p g e -> p (g e)"),
+                    in_=glob_grouped[:].rearrange("p g e t -> p (g e t)"),
+                )
+            if c == GLOB_CHUNK:
+                multiply_glob()
+                for tile in range(GLOB_CHUNK - FIRST_LAST_CHUNK):
+                    bias_tile(tile)
+            multiply_chunk(c)
+            if c >= GLOB_CHUNK:
+                bias_tile(c - FIRST_LAST_CHUNK)
 
-            if r == GLOB_ROUND:
-                glob_bank = bank_pool.tile([P, LATENT], F32, name="glob_bank", tag="bank")
-                for g in range(STREAM_GROUPS):
-                    group = X_GROUPS + g
+        for column in (0, HALF):
+            for m in range(EDGE_TILES):
+                last = bank_pool.tile([P, HALF], F32, name="last", tag="bank")
+                for group in LAST_GROUPS:
+                    codes, plane = last_codes[m, group]
                     nc.tensor.matmul_mx(
-                        out=glob_bank[:],
-                        lhsT=glob_codes[:, g, :].bitcast(FP8X4),
-                        lhsT_scale=glob_planes[:, g, :],
-                        rhs=w_tiles[group - group % ROUND_GROUPS][:, group % ROUND_GROUPS, :].bitcast(FP8X4),
-                        rhs_scale=w_plane(group),
-                        start=(g == 0),
-                        stop=(g == STREAM_GROUPS - 1),
+                        out=last[:],
+                        lhsT=codes.bitcast(FP8X4),
+                        lhsT_scale=plane,
+                        rhs=w_tiles[group, column].bitcast(FP8X4),
+                        rhs_scale=w_plane(group, column, HALF),
+                        start=(group == LAST_GROUPS[0]),
+                        stop=(group == LAST_GROUPS[1]),
                     )
+                summed = result_pool.tile([P, HALF], F32)
                 nc.vector.tensor_tensor(
-                    out=shared_row[:], in0=glob_bank[:], in1=b_all[:], op=mybir.AluOpType.add
+                    out=summed[:],
+                    in0=last[:],
+                    in1=partials[m][:, column : column + HALF],
+                    op=mybir.AluOpType.add,
+                )
+                result = result_pool.tile([P, HALF], F32)
+                nc.scalar.activation(
+                    out=result[:], in_=summed[:], func=mybir.ActivationFunctionType.Relu
+                )
+                nc.sync.dma_start(
+                    out=out[m * P : (m + 1) * P, column : column + HALF], in_=result[:]
                 )

@@ -38,7 +38,7 @@ def tile_edgemodel_pa_k_kernel(
     nc = tc.nc
     streams = (receiver, sender, edge_attr)
 
-    chunks = [(0, m, 2, g, 4) for g in (0, 4) for m in (0, 2)]
+    chunks = [(0, 0, EDGE_TILES, g, W_GROUPS) for g in range(0, STREAM_GROUPS, W_GROUPS)]
     chunks += [(s, m, 1, 0, STREAM_GROUPS) for s in (1, 2) for m in range(EDGE_TILES)]
 
     with ExitStack() as ctx:
@@ -113,11 +113,11 @@ def tile_edgemodel_pa_k_kernel(
                 column : column + columns,
             ]
 
-        load_x(0, pieces=2)
+        load_x(0, pieces=EDGE_TILES)
         load_scales(0)
         load_weight(0)
-        load_weight(2)
         load_x(1)
+        load_weight(2)
         nc.sync.dma_start(
             out=glob_rows[0:STREAM_GROUPS, :],
             in_=global_attr.rearrange("o (g c) -> (o g) c", g=STREAM_GROUPS),
@@ -126,9 +126,10 @@ def tile_edgemodel_pa_k_kernel(
         load_x(2)
         load_scales(1)
         load_weight(4)
-        load_weight(6)
         load_x(3)
+        load_weight(6)
         load_x(4)
+        load_x(5)
         load_scales(2)
         load_weight(8)
         load_weight(10)
@@ -137,7 +138,7 @@ def tile_edgemodel_pa_k_kernel(
         load_weight(14)
 
         def load_ahead(c):
-            if 5 <= c < len(chunks):
+            if 6 <= c < len(chunks):
                 load_x(c)
             if c == 8:
                 load_scales(4)
@@ -282,12 +283,13 @@ def tile_edgemodel_pa_k_kernel(
         shared_row = const.tile([P, LATENT], F32)
 
         for c in range(1, len(chunks)):
-            load_ahead(c + 4)
+            load_ahead(c + 5)
             if c + 1 < len(chunks):
                 sort_half(c + 1, 0)
                 sort_half(c + 1, 1)
-            quantise_half(c, 0)
-            quantise_half(c, 1)
+            if c != GLOB_CHUNK + 1:
+                quantise_half(c, 0)
+                quantise_half(c, 1)
             if c + 1 < len(chunks):
                 transpose_chunk(c + 1)
             if c == 3:
@@ -302,6 +304,8 @@ def tile_edgemodel_pa_k_kernel(
                     in_=glob_grouped[:].rearrange("p g e t -> p (g e t)"),
                 )
             if c == GLOB_CHUNK:
+                quantise_half(c + 1, 0)
+                quantise_half(c + 1, 1)
                 multiply_glob()
                 for tile in range(GLOB_CHUNK - FIRST_LAST_CHUNK):
                     bias_tile(tile)

@@ -21,12 +21,9 @@ HALF = LATENT // 2
 STREAM_GROUPS = D_STREAM // GROUP_K
 X_GROUPS = 3 * STREAM_GROUPS
 W_GROUPS = 2
-LAST_GROUPS = (X_GROUPS - 2, X_GROUPS - 1)
 PAIRS = 8
 BANK_PAIRS = 2
 X_BUFS = 6
-FIRST_LAST_CHUNK = 8
-GLOB_CHUNK = 10
 PLANES_PER_SET = 4
 
 FLOPS = 2 * EDGES * (4 * D_STREAM) * LATENT
@@ -80,18 +77,16 @@ def tile_edgemodel_pa_k_kernel(
                 )
             x_tiles[c] = x_sb
 
-        def load_weight(first_group, column=0, columns=LATENT):
-            w_sb = weights.tile(
-                [P, W_GROUPS, columns], U32, name="w%d_%d" % (first_group, column), align_bytes=64
-            )
+        def load_weight(first_group):
+            w_sb = weights.tile([P, W_GROUPS, LATENT], U32, name="w%d" % first_group, align_bytes=64)
             nc.sync.dma_start(
                 out=w_sb[:].bitcast(I32),
-                in_=W1_words[first_group : first_group + W_GROUPS, :, column : column + columns, :]
+                in_=W1_words[first_group : first_group + W_GROUPS]
                 .rearrange("g p n t -> p g (n t)")
                 .bitcast(I32),
             )
             for g in range(W_GROUPS):
-                w_tiles[first_group + g, column] = w_sb[:, g, :]
+                w_tiles[first_group + g] = w_sb[:, g, :]
 
         scale_words = W1_scales.bitcast(I32)
 
@@ -106,12 +101,8 @@ def tile_edgemodel_pa_k_kernel(
                     ],
                 )
 
-        def w_plane(group, column=0, columns=LATENT):
-            return w_planes[
-                4 * (group % PLANES_PER_SET) : P,
-                group // PLANES_PER_SET,
-                column : column + columns,
-            ]
+        def w_plane(group):
+            return w_planes[4 * (group % PLANES_PER_SET) : P, group // PLANES_PER_SET, :]
 
         load_x(0, pieces=EDGE_TILES)
         load_scales(0)
@@ -146,6 +137,7 @@ def tile_edgemodel_pa_k_kernel(
                 load_weight(18)
                 load_scales(5)
                 load_weight(20)
+                load_weight(22)
             if c == len(chunks) - 1:
                 load_scales(6)
                 load_weight(24)
@@ -153,24 +145,22 @@ def tile_edgemodel_pa_k_kernel(
                 load_scales(7)
                 load_weight(28)
                 load_weight(30)
-                load_weight(LAST_GROUPS[0], 0, HALF)
-                load_weight(LAST_GROUPS[0], HALF, HALF)
 
         sorted_tiles = {}
         quantised = {}
 
-        def sort_half(c, half):
-            if half == 0:
-                sorted_words = sorted_pool.tile([P, PAIRS, 2, P], F32)
-                sorted_tiles[c] = sorted_words
-            first = half * PAIRS // 2
+        def sort_chunk(c, parts=2):
+            sorted_words = sorted_pool.tile([P, PAIRS, 2, P], F32)
+            sorted_tiles[c] = sorted_words
             x_words = x_tiles[c][:].rearrange("p m c -> p (m c)").bitcast(F32)
-            nc.vector.tensor_copy(
-                out=sorted_tiles[c][:, first : first + PAIRS // 2],
-                in_=x_words[:, first * 2 * P : (first + PAIRS // 2) * 2 * P].rearrange(
-                    "p (i j u) -> p i u j", i=PAIRS // 2, u=2
-                ),
-            )
+            step = PAIRS // parts
+            for first in range(0, PAIRS, step):
+                nc.vector.tensor_copy(
+                    out=sorted_words[:, first : first + step],
+                    in_=x_words[:, first * 2 * P : (first + step) * 2 * P].rearrange(
+                        "p (i j u) -> p i u j", i=step, u=2
+                    ),
+                )
 
         def transpose_chunk(c):
             grouped = grouped_pool.tile([P, PAIRS, P * PACK], BF16, align_bytes=64)
@@ -207,7 +197,7 @@ def tile_edgemodel_pa_k_kernel(
         sums = [
             sums_pool.tile([P, LATENT], F32, name="sum%d" % m) for m in range(EDGE_TILES)
         ]
-        last_codes = {}
+        stops = {EDGE_TILES - 1: X_GROUPS - STREAM_GROUPS - 1}
 
         def multiply_chunk(c):
             s, m, tiles, g, groups = chunks[c]
@@ -215,17 +205,14 @@ def tile_edgemodel_pa_k_kernel(
             for pair in range(PAIRS):
                 tile = m + pair // groups
                 group = STREAM_GROUPS * s + g + pair % groups
-                if group in LAST_GROUPS:
-                    last_codes[tile, group] = (codes[:, pair, :], planes[:, pair, :])
-                    continue
                 nc.tensor.matmul_mx(
                     out=sums[tile][:],
                     lhsT=codes[:, pair, :].bitcast(FP8X4),
                     lhsT_scale=planes[:, pair, :],
-                    rhs=w_tiles[group, 0].bitcast(FP8X4),
+                    rhs=w_tiles[group].bitcast(FP8X4),
                     rhs_scale=w_plane(group),
                     start=(group == 0),
-                    stop=(group == LAST_GROUPS[0] - 1),
+                    stop=(group == stops.get(tile, X_GROUPS - 1)),
                 )
 
         def multiply_glob():
@@ -235,7 +222,7 @@ def tile_edgemodel_pa_k_kernel(
                     out=shared_bank[:],
                     lhsT=glob_codes[:, g, :].bitcast(FP8X4),
                     lhsT_scale=glob_planes[:, g, :],
-                    rhs=w_tiles[X_GROUPS + g, 0].bitcast(FP8X4),
+                    rhs=w_tiles[X_GROUPS + g].bitcast(FP8X4),
                     rhs_scale=w_plane(X_GROUPS + g),
                     start=(g == 0),
                     stop=(g == STREAM_GROUPS - 1),
@@ -244,23 +231,28 @@ def tile_edgemodel_pa_k_kernel(
                 out=shared_row[:], in0=shared_bank[:], in1=b_all[:], op=mybir.AluOpType.add
             )
 
-        partials = []
-
-        def bias_tile(m):
-            partial = const.tile([P, LATENT], F32, name="partial%d" % m)
-            nc.vector.tensor_tensor(
-                out=partial[:], in0=sums[m][:], in1=shared_row[:], op=mybir.AluOpType.add
+        def finish(summed, m, column, columns):
+            result = result_pool.tile([P, columns], F32, name="result%d" % columns)
+            nc.scalar.activation(
+                out=result[:], in_=summed[:], func=mybir.ActivationFunctionType.Relu
             )
-            partials.append(partial)
+            nc.sync.dma_start(
+                out=out[m * P : (m + 1) * P, column : column + columns], in_=result[:]
+            )
 
-        sort_half(0, 0)
-        sort_half(0, 1)
+        def finish_tile(m):
+            summed = result_pool.tile([P, LATENT], F32)
+            nc.vector.tensor_tensor(
+                out=summed[:], in0=sums[m][:], in1=shared_row[:], op=mybir.AluOpType.add
+            )
+            finish(summed, m, 0, LATENT)
+
+        sort_chunk(0, parts=EDGE_TILES)
         transpose_chunk(0)
         quantise_half(0, 0)
         quantise_half(0, 1)
         multiply_chunk(0)
-        sort_half(1, 0)
-        sort_half(1, 1)
+        sort_chunk(1)
 
         b_bank = bank_pool.tile([P, LATENT], F32, name="b_bank", tag="bank")
         nc.tensor.matmul(out=b_bank[:], lhsT=ones[:], rhs=b_rows[:], start=True, stop=True)
@@ -282,16 +274,13 @@ def tile_edgemodel_pa_k_kernel(
         glob_planes = const.tile([P, STREAM_GROUPS, P], U8, align_bytes=64)
         shared_row = const.tile([P, LATENT], F32)
 
-        for c in range(1, len(chunks)):
+        last = len(chunks) - 1
+        for c in range(1, last):
             load_ahead(c + 5)
-            if c + 1 < len(chunks):
-                sort_half(c + 1, 0)
-                sort_half(c + 1, 1)
-            if c != GLOB_CHUNK + 1:
-                quantise_half(c, 0)
-                quantise_half(c, 1)
-            if c + 1 < len(chunks):
-                transpose_chunk(c + 1)
+            sort_chunk(c + 1)
+            quantise_half(c, 0)
+            quantise_half(c, 1)
+            transpose_chunk(c + 1)
             if c == 3:
                 nc.vector.tensor_copy(
                     out=glob_grouped[:],
@@ -303,41 +292,42 @@ def tile_edgemodel_pa_k_kernel(
                     scales=glob_planes[:].rearrange("p g e -> p (g e)"),
                     in_=glob_grouped[:].rearrange("p g e t -> p (g e t)"),
                 )
-            if c == GLOB_CHUNK:
-                quantise_half(c + 1, 0)
-                quantise_half(c + 1, 1)
+            if c == last - 1:
+                quantise_half(last, 0)
+                quantise_half(last, 1)
                 multiply_glob()
-                for tile in range(GLOB_CHUNK - FIRST_LAST_CHUNK):
-                    bias_tile(tile)
-            multiply_chunk(c)
-            if c >= GLOB_CHUNK:
-                bias_tile(c - FIRST_LAST_CHUNK)
-
-        for column in (0, HALF):
-            for m in range(EDGE_TILES):
-                last = bank_pool.tile([P, HALF], F32, name="last", tag="bank")
-                for group in LAST_GROUPS:
-                    codes, plane = last_codes[m, group]
-                    nc.tensor.matmul_mx(
-                        out=last[:],
-                        lhsT=codes.bitcast(FP8X4),
-                        lhsT_scale=plane,
-                        rhs=w_tiles[group, column].bitcast(FP8X4),
-                        rhs_scale=w_plane(group, column, HALF),
-                        start=(group == LAST_GROUPS[0]),
-                        stop=(group == LAST_GROUPS[1]),
-                    )
-                summed = result_pool.tile([P, HALF], F32)
+                partial = const.tile([P, LATENT], F32)
                 nc.vector.tensor_tensor(
-                    out=summed[:],
-                    in0=last[:],
-                    in1=partials[m][:, column : column + HALF],
+                    out=partial[:],
+                    in0=sums[EDGE_TILES - 1][:],
+                    in1=shared_row[:],
                     op=mybir.AluOpType.add,
                 )
-                result = result_pool.tile([P, HALF], F32)
-                nc.scalar.activation(
-                    out=result[:], in_=summed[:], func=mybir.ActivationFunctionType.Relu
+                for m in range(EDGE_TILES - 2):
+                    finish_tile(m)
+            multiply_chunk(c)
+        finish_tile(EDGE_TILES - 2)
+
+        codes, planes = quantised[last][1:]
+        for column in (0, HALF):
+            columns = slice(column, column + HALF)
+            half_bank = bank_pool.tile([P, HALF], F32, name="half_bank", tag="bank")
+            for g in range(STREAM_GROUPS):
+                group = X_GROUPS - STREAM_GROUPS + g
+                nc.tensor.matmul_mx(
+                    out=half_bank[:],
+                    lhsT=codes[:, g, :].bitcast(FP8X4),
+                    lhsT_scale=planes[:, g, :],
+                    rhs=w_tiles[group][:, columns].bitcast(FP8X4),
+                    rhs_scale=w_plane(group)[:, columns],
+                    start=(g == 0),
+                    stop=(g == STREAM_GROUPS - 1),
                 )
-                nc.sync.dma_start(
-                    out=out[m * P : (m + 1) * P, column : column + HALF], in_=result[:]
-                )
+            summed_half = result_pool.tile([P, HALF], F32)
+            nc.vector.tensor_tensor(
+                out=summed_half[:],
+                in0=half_bank[:],
+                in1=partial[:, columns],
+                op=mybir.AluOpType.add,
+            )
+            finish(summed_half, EDGE_TILES - 1, column, HALF)

@@ -24,6 +24,7 @@ W_GROUPS = 2
 PAIRS = 8
 BANK_PAIRS = 2
 X_BUFS = 6
+SETS = 8
 PLANES_PER_SET = 4
 
 FLOPS = 2 * EDGES * (4 * D_STREAM) * LATENT
@@ -52,7 +53,7 @@ def tile_edgemodel_pa_k_kernel(
 
         identity = const.tile([P, P], F32)
         make_identity(nc, identity[:])
-        w_planes = const.tile([P, 4 * STREAM_GROUPS // PLANES_PER_SET, LATENT], U8, align_bytes=64)
+        w_planes = const.tile([P, SETS, LATENT], U8, align_bytes=64)
         nc.vector.memset(w_planes[:].bitcast(I32), 0)
         ones = const.tile([P, P], BF16)
         nc.vector.memset(ones[:], 1.0)
@@ -90,8 +91,10 @@ def tile_edgemodel_pa_k_kernel(
 
         scale_words = W1_scales.bitcast(I32)
 
-        def load_scales(s):
-            for quadrant in range(4):
+        scale_loads = [(s, quadrant) for s in range(SETS) for quadrant in range(4)]
+
+        def load_scales(count):
+            for s, quadrant in scale_loads[:count]:
                 nc.sync.dma_start(
                     out=w_planes[32 * quadrant : 32 * quadrant + 16, s, :].bitcast(I32),
                     in_=scale_words[
@@ -100,51 +103,44 @@ def tile_edgemodel_pa_k_kernel(
                         :,
                     ],
                 )
+            scale_loads[:] = scale_loads[count:]
 
         def w_plane(group):
             return w_planes[4 * (group % PLANES_PER_SET) : P, group // PLANES_PER_SET, :]
 
+        def load(kind, i):
+            (load_x if kind == "x" else load_weight)(i)
+            load_scales(1)
+
         load_x(0, pieces=EDGE_TILES)
-        load_scales(0)
-        load_weight(0)
-        load_x(1)
-        load_weight(2)
+        load_scales(4)
+        load("w", 0)
+        load("x", 1)
+        load("w", 2)
         nc.sync.dma_start(
             out=glob_rows[0:STREAM_GROUPS, :],
             in_=global_attr.rearrange("o (g c) -> (o g) c", g=STREAM_GROUPS),
         )
         nc.sync.dma_start(out=b_rows[0:1, :], in_=b1.unsqueeze(0))
-        load_x(2)
-        load_scales(1)
-        load_weight(4)
-        load_x(3)
-        load_weight(6)
-        load_x(4)
-        load_x(5)
-        load_scales(2)
-        load_weight(8)
-        load_weight(10)
-        load_scales(3)
-        load_weight(12)
-        load_weight(14)
+        load("x", 2)
+        load("w", 4)
+        load("x", 3)
+        load("w", 6)
+        load("x", 4)
+        load("x", 5)
+        for group in range(8, 16, W_GROUPS):
+            load("w", group)
 
         def load_ahead(c):
             if 6 <= c < len(chunks):
-                load_x(c)
+                load("x", c)
             if c == 8:
-                load_scales(4)
-                load_weight(16)
-                load_weight(18)
-                load_scales(5)
-                load_weight(20)
-                load_weight(22)
+                for group in range(16, 24, W_GROUPS):
+                    load("w", group)
             if c == len(chunks) - 1:
-                load_scales(6)
-                load_weight(24)
-                load_weight(26)
-                load_scales(7)
-                load_weight(28)
-                load_weight(30)
+                for group in range(24, 32, W_GROUPS):
+                    load("w", group)
+                load_scales(len(scale_loads))
 
         sorted_tiles = {}
         quantised = {}

@@ -21,6 +21,7 @@ HALF = LATENT // 2
 STREAM_GROUPS = D_STREAM // GROUP_K
 X_GROUPS = 3 * STREAM_GROUPS
 W_GROUPS = 2
+LATE_CHUNK = 6
 PAIRS = 8
 BANK_PAIRS = 2
 X_BUFS = 6
@@ -134,8 +135,9 @@ def tile_edgemodel_pa_k_kernel(
         def load_ahead(c):
             if 6 <= c < len(chunks):
                 load("x", c)
-            if c == 8:
-                for group in range(16, 24, W_GROUPS):
+            if c in (8, 9):
+                first = 2 * STREAM_GROUPS + (c - 8) * STREAM_GROUPS // 2
+                for group in range(first, first + STREAM_GROUPS // 2, W_GROUPS):
                     load("w", group)
             if c == len(chunks) - 1:
                 for group in range(24, 32, W_GROUPS):
@@ -273,6 +275,13 @@ def tile_edgemodel_pa_k_kernel(
         last = len(chunks) - 1
         for c in range(1, last):
             load_ahead(c + 5)
+            if c + 1 == LATE_CHUNK:
+                quantise_half(c, 0)
+                quantise_half(c, 1)
+                multiply_chunk(c)
+                sort_chunk(c + 1)
+                transpose_chunk(c + 1)
+                continue
             sort_chunk(c + 1)
             quantise_half(c, 0)
             quantise_half(c, 1)

@@ -17,7 +17,7 @@ EDGES = 512
 EDGE_TILES = EDGES // P
 D_STREAM = 4096
 LATENT = 512
-HALF = LATENT // 2
+LAST_PIECES = (256, 128, 128)
 STREAM_GROUPS = D_STREAM // GROUP_K
 X_GROUPS = 3 * STREAM_GROUPS
 W_GROUPS = 2
@@ -37,7 +37,8 @@ def tile_edgemodel_pa_k_kernel(
     nc = tc.nc
     streams = (receiver, sender, edge_attr)
 
-    chunks = [(0, 0, EDGE_TILES, g, W_GROUPS) for g in range(0, STREAM_GROUPS, W_GROUPS)]
+    chunks = [(0, 0, EDGE_TILES, g, W_GROUPS) for g in (0, W_GROUPS)]
+    chunks += [(0, m, 2, 2 * W_GROUPS, 2 * W_GROUPS) for m in (0, 2)]
     chunks += [(s, m, 1, 0, STREAM_GROUPS) for s in (1, 2) for m in range(EDGE_TILES)]
 
     with ExitStack() as ctx:
@@ -109,23 +110,23 @@ def tile_edgemodel_pa_k_kernel(
         def w_plane(group):
             return w_planes[4 * (group % PLANES_PER_SET) : P, group // PLANES_PER_SET, :]
 
-        def load(kind, i):
+        def load(kind, i, scales=1):
             (load_x if kind == "x" else load_weight)(i)
-            load_scales(1)
+            load_scales(scales)
 
         load_x(0, pieces=EDGE_TILES)
         load_scales(4)
         load("w", 0)
         load("x", 1)
-        load("w", 2)
+        load("x", 2)
         nc.sync.dma_start(
             out=glob_rows[0:STREAM_GROUPS, :],
             in_=global_attr.rearrange("o (g c) -> (o g) c", g=STREAM_GROUPS),
         )
         nc.sync.dma_start(out=b_rows[0:1, :], in_=b1.unsqueeze(0))
-        load("x", 2)
-        load("w", 4)
+        load("w", 2)
         load("x", 3)
+        load("w", 4)
         load("w", 6)
         load("x", 4)
         load("x", 5)
@@ -134,7 +135,7 @@ def tile_edgemodel_pa_k_kernel(
 
         def load_ahead(c):
             if 6 <= c < len(chunks):
-                load("x", c)
+                load("x", c, scales=2 if c > 9 else 1)
             if c in (8, 9):
                 first = 2 * STREAM_GROUPS + (c - 8) * STREAM_GROUPS // 2
                 for group in range(first, first + STREAM_GROUPS // 2, W_GROUPS):
@@ -142,7 +143,6 @@ def tile_edgemodel_pa_k_kernel(
             if c == len(chunks) - 1:
                 for group in range(24, 32, W_GROUPS):
                     load("w", group)
-                load_scales(len(scale_loads))
 
         sorted_tiles = {}
         quantised = {}
@@ -251,21 +251,6 @@ def tile_edgemodel_pa_k_kernel(
         quantise_half(0, 1)
         multiply_chunk(0)
         sort_chunk(1)
-
-        b_bank = bank_pool.tile([P, LATENT], F32, name="b_bank", tag="bank")
-        nc.tensor.matmul(out=b_bank[:], lhsT=ones[:], rhs=b_rows[:], start=True, stop=True)
-        glob_bank = bank_pool.tile([P, 2, P], F32, name="glob_bank", tag="bank")
-        for u in range(2):
-            nc.tensor.transpose(
-                glob_bank[:, u, :], glob_rows[:].bitcast(F32)[:, u::2], identity[:]
-            )
-        b_all = const.tile([P, LATENT], F32)
-        nc.scalar.copy(out=b_all[:], in_=b_bank[:])
-        glob_sb = const.tile([P, STREAM_GROUPS, PACK], BF16)
-        nc.scalar.copy(
-            out=glob_sb[:].rearrange("p g t -> p (g t)").bitcast(F32).rearrange("p (g u) -> p g u", u=2),
-            in_=glob_bank[:, :, 0:STREAM_GROUPS].rearrange("p u g -> p g u"),
-        )
         transpose_chunk(1)
         glob_grouped = const.tile([P, STREAM_GROUPS, P, PACK], BF16, align_bytes=64)
         glob_codes = const.tile([P, STREAM_GROUPS, P], U32, align_bytes=64)
@@ -286,6 +271,21 @@ def tile_edgemodel_pa_k_kernel(
             quantise_half(c, 0)
             quantise_half(c, 1)
             transpose_chunk(c + 1)
+            if c == 1:
+                b_bank = bank_pool.tile([P, LATENT], F32, name="b_bank", tag="bank")
+                nc.tensor.matmul(out=b_bank[:], lhsT=ones[:], rhs=b_rows[:], start=True, stop=True)
+                glob_bank = bank_pool.tile([P, 2, P], F32, name="glob_bank", tag="bank")
+                for u in range(2):
+                    nc.tensor.transpose(
+                        glob_bank[:, u, :], glob_rows[:].bitcast(F32)[:, u::2], identity[:]
+                    )
+                b_all = const.tile([P, LATENT], F32)
+                nc.scalar.copy(out=b_all[:], in_=b_bank[:])
+                glob_sb = const.tile([P, STREAM_GROUPS, PACK], BF16)
+                nc.scalar.copy(
+                    out=glob_sb[:].rearrange("p g t -> p (g t)").bitcast(F32).rearrange("p (g u) -> p g u", u=2),
+                    in_=glob_bank[:, :, 0:STREAM_GROUPS].rearrange("p u g -> p g u"),
+                )
             if c == 3:
                 nc.vector.tensor_copy(
                     out=glob_grouped[:],
@@ -314,13 +314,14 @@ def tile_edgemodel_pa_k_kernel(
         finish_tile(EDGE_TILES - 2)
 
         codes, planes = quantised[last][1:]
-        for column in (0, HALF):
-            columns = slice(column, column + HALF)
-            half_bank = bank_pool.tile([P, HALF], F32, name="half_bank", tag="bank")
+        column = 0
+        for width in LAST_PIECES:
+            columns = slice(column, column + width)
+            piece_bank = bank_pool.tile([P, width], F32, name="piece_bank", tag="bank")
             for g in range(STREAM_GROUPS):
                 group = X_GROUPS - STREAM_GROUPS + g
                 nc.tensor.matmul_mx(
-                    out=half_bank[:],
+                    out=piece_bank[:],
                     lhsT=codes[:, g, :].bitcast(FP8X4),
                     lhsT_scale=planes[:, g, :],
                     rhs=w_tiles[group][:, columns].bitcast(FP8X4),
@@ -328,11 +329,12 @@ def tile_edgemodel_pa_k_kernel(
                     start=(g == 0),
                     stop=(g == STREAM_GROUPS - 1),
                 )
-            summed_half = result_pool.tile([P, HALF], F32)
+            summed_piece = result_pool.tile([P, width], F32, name="summed%d" % width)
             nc.vector.tensor_tensor(
-                out=summed_half[:],
-                in0=half_bank[:],
+                out=summed_piece[:],
+                in0=piece_bank[:],
                 in1=partial[:, columns],
                 op=mybir.AluOpType.add,
             )
-            finish(summed_half, EDGE_TILES - 1, column, HALF)
+            finish(summed_piece, EDGE_TILES - 1, column, width)
+            column += width

from contextlib import ExitStack

import concourse.mybir as mybir
from concourse.masks import make_identity

F32 = mybir.dt.float32
BF16 = mybir.dt.bfloat16
I32 = mybir.dt.int32
U32 = mybir.dt.uint32
U8 = mybir.dt.uint8
FP8X4 = mybir.dt.float8_e4m3fn_x4

P = 128
PACK = 4
GROUP_K = P * PACK
EDGES = 512
EDGE_TILES = EDGES // P
D_STREAM = 4096
LATENT = 512
LAST_PIECES = (256, 128, 128)
STREAM_GROUPS = D_STREAM // GROUP_K
X_GROUPS = 3 * STREAM_GROUPS
W_GROUPS = 2
LATE_CHUNK = 6
PAIRS = 8
BANK_PAIRS = 2
X_BUFS = 6
SETS = 8
PLANES_PER_SET = 4

FLOPS = 2 * EDGES * (4 * D_STREAM) * LATENT


def tile_edgemodel_pa_k_kernel(
    tc, receiver, sender, edge_attr, global_attr, W1_words, W1_scales, b1, out
):
    nc = tc.nc
    streams = (receiver, sender, edge_attr)

    chunks = [(0, 0, EDGE_TILES, g, W_GROUPS) for g in (0, W_GROUPS)]
    chunks += [(0, m, 2, 2 * W_GROUPS, 2 * W_GROUPS) for m in (0, 2)]
    chunks += [(s, m, 1, 0, STREAM_GROUPS) for s in (1, 2) for m in range(EDGE_TILES)]

    with ExitStack() as ctx:
        const = ctx.enter_context(tc.tile_pool(name="const", bufs=1))
        weights = ctx.enter_context(tc.tile_pool(name="weights", bufs=1))
        x_pool = ctx.enter_context(tc.tile_pool(name="x", bufs=X_BUFS))
        sorted_pool = ctx.enter_context(tc.tile_pool(name="sorted", bufs=2))
        grouped_pool = ctx.enter_context(tc.tile_pool(name="grouped", bufs=2))
        quantised_pool = ctx.enter_context(tc.tile_pool(name="quantised", bufs=6))
        result_pool = ctx.enter_context(tc.tile_pool(name="result", bufs=4))
        sums_pool = ctx.enter_context(tc.psum_pool(name="sums", bufs=1))
        bank_pool = ctx.enter_context(tc.psum_pool(name="bank", bufs=4))
        ctx.enter_context(tc.manual_schedule())

        identity = const.tile([P, P], F32)
        make_identity(nc, identity[:])
        w_planes = const.tile([P, SETS, LATENT], U8, align_bytes=64)
        nc.vector.memset(w_planes[:].bitcast(I32), 0)
        ones = const.tile([P, P], BF16)
        nc.vector.memset(ones[:], 1.0)
        b_rows = const.tile([P, LATENT], BF16)
        nc.vector.memset(b_rows[:].bitcast(I32), 0)
        glob_rows = const.tile([P, GROUP_K], BF16)
        nc.vector.memset(glob_rows[:].bitcast(I32), 0)

        x_tiles = {}
        w_tiles = {}

        def load_x(c, pieces=1):
            s, m, tiles, g, groups = chunks[c]
            x_sb = x_pool.tile([P, tiles, groups * GROUP_K], BF16)
            step = tiles // pieces
            for i in range(0, tiles, step):
                nc.sync.dma_start(
                    out=x_sb[:, i : i + step, :],
                    in_=streams[s][
                        (m + i) * P : (m + i + step) * P, g * GROUP_K : (g + groups) * GROUP_K
                    ].rearrange("(m p) c -> p m c", p=P),
                )
            x_tiles[c] = x_sb

        def load_weight(first_group):
            w_sb = weights.tile([P, W_GROUPS, LATENT], U32, name="w%d" % first_group, align_bytes=64)
            nc.sync.dma_start(
                out=w_sb[:].bitcast(I32),
                in_=W1_words[first_group : first_group + W_GROUPS]
                .rearrange("g p n t -> p g (n t)")
                .bitcast(I32),
            )
            for g in range(W_GROUPS):
                w_tiles[first_group + g] = w_sb[:, g, :]

        scale_words = W1_scales.bitcast(I32)

        scale_loads = [(s, quadrant) for s in range(SETS) for quadrant in range(4)]

        def load_scales(count):
            for s, quadrant in scale_loads[:count]:
                nc.sync.dma_start(
                    out=w_planes[32 * quadrant : 32 * quadrant + 16, s, :].bitcast(I32),
                    in_=scale_words[
                        PLANES_PER_SET * s : PLANES_PER_SET * (s + 1),
                        4 * quadrant : 4 * quadrant + 4,
                        :,
                    ],
                )
            scale_loads[:] = scale_loads[count:]

        def w_plane(group):
            return w_planes[4 * (group % PLANES_PER_SET) : P, group // PLANES_PER_SET, :]

        def load(kind, i, scales=1):
            (load_x if kind == "x" else load_weight)(i)
            load_scales(scales)

        load_x(0, pieces=EDGE_TILES)
        load_scales(4)
        load("w", 0)
        load("x", 1)
        load("x", 2)
        nc.sync.dma_start(
            out=glob_rows[0:STREAM_GROUPS, :],
            in_=global_attr.rearrange("o (g c) -> (o g) c", g=STREAM_GROUPS),
        )
        nc.sync.dma_start(out=b_rows[0:1, :], in_=b1.unsqueeze(0))
        load("w", 2)
        load("x", 3)
        load("w", 4)
        load("w", 6)
        load("x", 4)
        load("x", 5)
        for group in range(8, 16, W_GROUPS):
            load("w", group)

        def load_ahead(c):
            if 6 <= c < len(chunks):
                load("x", c, scales=2 if c > 9 else 1)
            if c in (8, 9):
                first = 2 * STREAM_GROUPS + (c - 8) * STREAM_GROUPS // 2
                for group in range(first, first + STREAM_GROUPS // 2, W_GROUPS):
                    load("w", group)
            if c == len(chunks) - 1:
                for group in range(24, 32, W_GROUPS):
                    load("w", group)

        sorted_tiles = {}
        quantised = {}

        def sort_chunk(c, parts=2):
            sorted_words = sorted_pool.tile([P, PAIRS, 2, P], F32)
            sorted_tiles[c] = sorted_words
            x_words = x_tiles[c][:].rearrange("p m c -> p (m c)").bitcast(F32)
            step = PAIRS // parts
            for first in range(0, PAIRS, step):
                nc.vector.tensor_copy(
                    out=sorted_words[:, first : first + step],
                    in_=x_words[:, first * 2 * P : (first + step) * 2 * P].rearrange(
                        "p (i j u) -> p i u j", i=step, u=2
                    ),
                )

        def transpose_chunk(c):
            grouped = grouped_pool.tile([P, PAIRS, P * PACK], BF16, align_bytes=64)
            banks = []
            for first in range(0, PAIRS, BANK_PAIRS):
                bank = bank_pool.tile([P, BANK_PAIRS, 2, P], F32, name="bank")
                for i in range(BANK_PAIRS):
                    for u in range(2):
                        nc.tensor.transpose(
                            bank[:, i, u, :], sorted_tiles[c][:, first + i, u, :], identity[:]
                        )
                banks.append(bank)
            for i, bank in enumerate(banks):
                nc.scalar.copy(
                    out=grouped[:, BANK_PAIRS * i : BANK_PAIRS * (i + 1), :]
                    .rearrange("p i c -> p (i c)")
                    .bitcast(F32)
                    .rearrange("p (i e u) -> p i e u", i=BANK_PAIRS, u=2),
                    in_=bank[:].rearrange("p i u e -> p i e u"),
                )
            codes = quantised_pool.tile([P, PAIRS, P], U32, align_bytes=64)
            planes = quantised_pool.tile([P, PAIRS, P], U8, align_bytes=64)
            quantised[c] = (grouped, codes, planes)

        def quantise_half(c, half):
            grouped, codes, planes = quantised[c]
            part = slice(half * PAIRS // 2, (half + 1) * PAIRS // 2)
            nc.vector.quantize_mx(
                out=codes[:, part].rearrange("p i e -> p (i e)").bitcast(FP8X4),
                scales=planes[:, part].rearrange("p i e -> p (i e)"),
                in_=grouped[:, part, :].rearrange("p i c -> p (i c)"),
            )

        sums = [
            sums_pool.tile([P, LATENT], F32, name="sum%d" % m) for m in range(EDGE_TILES)
        ]
        stops = {EDGE_TILES - 1: X_GROUPS - STREAM_GROUPS - 1}

        def multiply_chunk(c):
            s, m, tiles, g, groups = chunks[c]
            codes, planes = quantised[c][1:]
            for pair in range(PAIRS):
                tile = m + pair // groups
                group = STREAM_GROUPS * s + g + pair % groups
                nc.tensor.matmul_mx(
                    out=sums[tile][:],
                    lhsT=codes[:, pair, :].bitcast(FP8X4),
                    lhsT_scale=planes[:, pair, :],
                    rhs=w_tiles[group].bitcast(FP8X4),
                    rhs_scale=w_plane(group),
                    start=(group == 0),
                    stop=(group == stops.get(tile, X_GROUPS - 1)),
                )

        def multiply_glob():
            shared_bank = bank_pool.tile([P, LATENT], F32, name="shared_bank", tag="bank")
            for g in range(STREAM_GROUPS):
                nc.tensor.matmul_mx(
                    out=shared_bank[:],
                    lhsT=glob_codes[:, g, :].bitcast(FP8X4),
                    lhsT_scale=glob_planes[:, g, :],
                    rhs=w_tiles[X_GROUPS + g].bitcast(FP8X4),
                    rhs_scale=w_plane(X_GROUPS + g),
                    start=(g == 0),
                    stop=(g == STREAM_GROUPS - 1),
                )
            nc.vector.tensor_tensor(
                out=shared_row[:], in0=shared_bank[:], in1=b_all[:], op=mybir.AluOpType.add
            )

        def finish(summed, m, column, columns):
            result = result_pool.tile([P, columns], F32, name="result%d" % columns)
            nc.scalar.activation(
                out=result[:], in_=summed[:], func=mybir.ActivationFunctionType.Relu
            )
            nc.sync.dma_start(
                out=out[m * P : (m + 1) * P, column : column + columns], in_=result[:]
            )

        def finish_tile(m):
            summed = result_pool.tile([P, LATENT], F32)
            nc.vector.tensor_tensor(
                out=summed[:], in0=sums[m][:], in1=shared_row[:], op=mybir.AluOpType.add
            )
            finish(summed, m, 0, LATENT)

        sort_chunk(0, parts=EDGE_TILES)
        transpose_chunk(0)
        quantise_half(0, 0)
        quantise_half(0, 1)
        multiply_chunk(0)
        sort_chunk(1)
        transpose_chunk(1)
        glob_grouped = const.tile([P, STREAM_GROUPS, P, PACK], BF16, align_bytes=64)
        glob_codes = const.tile([P, STREAM_GROUPS, P], U32, align_bytes=64)
        glob_planes = const.tile([P, STREAM_GROUPS, P], U8, align_bytes=64)
        shared_row = const.tile([P, LATENT], F32)

        last = len(chunks) - 1
        for c in range(1, last):
            load_ahead(c + 5)
            if c + 1 == LATE_CHUNK:
                quantise_half(c, 0)
                quantise_half(c, 1)
                multiply_chunk(c)
                sort_chunk(c + 1)
                transpose_chunk(c + 1)
                continue
            sort_chunk(c + 1)
            quantise_half(c, 0)
            quantise_half(c, 1)
            transpose_chunk(c + 1)
            if c == 1:
                b_bank = bank_pool.tile([P, LATENT], F32, name="b_bank", tag="bank")
                nc.tensor.matmul(out=b_bank[:], lhsT=ones[:], rhs=b_rows[:], start=True, stop=True)
                glob_bank = bank_pool.tile([P, 2, P], F32, name="glob_bank", tag="bank")
                for u in range(2):
                    nc.tensor.transpose(
                        glob_bank[:, u, :], glob_rows[:].bitcast(F32)[:, u::2], identity[:]
                    )
                b_all = const.tile([P, LATENT], F32)
                nc.scalar.copy(out=b_all[:], in_=b_bank[:])
                glob_sb = const.tile([P, STREAM_GROUPS, PACK], BF16)
                nc.scalar.copy(
                    out=glob_sb[:].rearrange("p g t -> p (g t)").bitcast(F32).rearrange("p (g u) -> p g u", u=2),
                    in_=glob_bank[:, :, 0:STREAM_GROUPS].rearrange("p u g -> p g u"),
                )
            if c == 3:
                nc.vector.tensor_copy(
                    out=glob_grouped[:],
                    in_=glob_sb[:].unsqueeze(2).to_broadcast([P, STREAM_GROUPS, P, PACK]),
                )
            if c == 4:
                nc.vector.quantize_mx(
                    out=glob_codes[:].rearrange("p g e -> p (g e)").bitcast(FP8X4),
                    scales=glob_planes[:].rearrange("p g e -> p (g e)"),
                    in_=glob_grouped[:].rearrange("p g e t -> p (g e t)"),
                )
            if c == last - 1:
                quantise_half(last, 0)
                quantise_half(last, 1)
                multiply_glob()
                partial = const.tile([P, LATENT], F32)
                nc.vector.tensor_tensor(
                    out=partial[:],
                    in0=sums[EDGE_TILES - 1][:],
                    in1=shared_row[:],
                    op=mybir.AluOpType.add,
                )
                for m in range(EDGE_TILES - 2):
                    finish_tile(m)
            multiply_chunk(c)
        finish_tile(EDGE_TILES - 2)

        codes, planes = quantised[last][1:]
        column = 0
        for width in LAST_PIECES:
            columns = slice(column, column + width)
            piece_bank = bank_pool.tile([P, width], F32, name="piece_bank", tag="bank")
            for g in range(STREAM_GROUPS):
                group = X_GROUPS - STREAM_GROUPS + g
                nc.tensor.matmul_mx(
                    out=piece_bank[:],
                    lhsT=codes[:, g, :].bitcast(FP8X4),
                    lhsT_scale=planes[:, g, :],
                    rhs=w_tiles[group][:, columns].bitcast(FP8X4),
                    rhs_scale=w_plane(group)[:, columns],
                    start=(g == 0),
                    stop=(g == STREAM_GROUPS - 1),
                )
            summed_piece = result_pool.tile([P, width], F32, name="summed%d" % width)
            nc.vector.tensor_tensor(
                out=summed_piece[:],
                in0=piece_bank[:],
                in1=partial[:, columns],
                op=mybir.AluOpType.add,
            )
            finish(summed_piece, EDGE_TILES - 1, column, width)
            column += width
